import numpy as np
import ml_dtypes

BF16 = ml_dtypes.bfloat16


def bf(x):
    return np.asarray(x, np.float32).astype(BF16)


def f32(x):
    return np.asarray(x, np.float32)


def f64(x):
    return np.asarray(x).astype(np.float64)


def striped(idx):
    return np.tile(idx.reshape(-1, 16).T, (8, 1))


H, D, HALF, C, S, N = 8, 128, 64, 1024, 1024, 128


def setup_inputs():
    return {"base": f32(np.random.standard_normal((C, S))), "k_new": f32(np.random.standard_normal((C, N))), "cos_t": f32(np.random.uniform(size=(HALF, N))), "sin_t": f32(np.random.uniform(size=(HALF, N))), "offs": striped(np.random.permutation(S)[:N])}


def reference(base, k_new, cos_t, sin_t, offs):
    idx = offs[:16].T.reshape(-1)
    kh = f64(k_new).reshape(H, D, N)
    fc = np.concatenate([f64(cos_t), f64(cos_t)], axis=0)[None]
    fs = np.concatenate([f64(sin_t), f64(sin_t)], axis=0)[None]
    rot = np.concatenate([-kh[:, HALF:], kh[:, :HALF]], axis=1)
    out = f64(base).copy()
    out[:, idx] = (kh * fc + rot * fs).reshape(C, N)
    return out

@@ -1,0 +1,51 @@
+import concourse.mybir as mybir
+
+F32 = mybir.dt.float32
+U16 = mybir.dt.uint16
+MULT = mybir.AluOpType.mult
+ADD = mybir.AluOpType.add
+
+H = 8
+D = 128
+HALF = 64
+S = 1024
+N = 128
+
+
+def tile_lmattention_kernel(tc, base, k_new, cos_t, sin_t, offs, out):
+    nc = tc.nc
+    k_by_head = k_new.rearrange("(h d) j -> d h j", d=D)
+
+    with (
+        tc.tile_pool(name="held", bufs=1) as held,
+        tc.tile_pool(name="cache", bufs=H) as cache,
+        tc.tile_pool(name="products", bufs=2) as products,
+    ):
+        offsets = held.tile([D, N // 16], U16, name="offsets")
+        nc.sync.dma_start(offsets[:], offs)
+
+        k_straight = held.tile([D, H, N], F32, name="k_straight")
+        nc.sync.dma_start(k_straight[:], k_by_head)
+        k_swapped = held.tile([D, H, N], F32, name="k_swapped")
+        nc.scalar.dma_start(k_swapped[0:HALF], k_by_head[HALF:D])
+        nc.scalar.dma_start(k_swapped[HALF:D], k_by_head[0:HALF])
+
+        cos_both = held.tile([D, N], F32, name="cos_both")
+        sin_both = held.tile([D, N], F32, name="sin_both")
+        for low in (0, HALF):
+            nc.scalar.dma_start(cos_both[low : low + HALF], cos_t)
+            nc.scalar.dma_start(sin_both[low : low + HALF], sin_t)
+        nc.vector.tensor_scalar_mul(sin_both[0:HALF], sin_both[0:HALF], -1.0)
+
+        for h in range(H):
+            rows = slice(h * D, (h + 1) * D)
+            window = cache.tile([D, S], F32, name="window")
+            nc.sync.dma_start(window[:], base[rows, :])
+
+            by_cos = products.tile([D, N], F32, name="by_cos")
+            nc.vector.tensor_tensor(by_cos[:], k_straight[:, h, :], cos_both[:], MULT)
+            by_sin = products.tile([D, N], F32, name="by_sin")
+            nc.vector.tensor_tensor(by_sin[:], k_swapped[:, h, :], sin_both[:], MULT)
+
+            nc.vector.tensor_tensor(window[:].indirect(offsets[:]), by_cos[:], by_sin[:], ADD)
+            nc.scalar.dma_start(out[rows, :], window[:])

@@ -1,4 +1,5 @@
 import concourse.mybir as mybir
+from concourse.masks import make_identity
 
 F32 = mybir.dt.float32
 U16 = mybir.dt.uint16
@@ -14,38 +15,43 @@ N = 128
 
 def tile_lmattention_kernel(tc, base, k_new, cos_t, sin_t, offs, out):
     nc = tc.nc
-    k_by_head = k_new.rearrange("(h d) j -> d h j", d=D)
 
     with (
         tc.tile_pool(name="held", bufs=1) as held,
         tc.tile_pool(name="cache", bufs=H) as cache,
         tc.tile_pool(name="products", bufs=2) as products,
+        tc.psum_pool(name="turned", bufs=2) as turned,
     ):
         offsets = held.tile([D, N // 16], U16, name="offsets")
         nc.sync.dma_start(offsets[:], offs)
 
-        k_straight = held.tile([D, H, N], F32, name="k_straight")
-        nc.sync.dma_start(k_straight[:], k_by_head)
-        k_swapped = held.tile([D, H, N], F32, name="k_swapped")
-        nc.scalar.dma_start(k_swapped[0:HALF], k_by_head[HALF:D])
-        nc.scalar.dma_start(k_swapped[HALF:D], k_by_head[0:HALF])
+        keys = held.tile([D, H, N], F32, name="keys")
+        nc.sync.dma_start(keys[:], k_new.rearrange("(h d) j -> d h j", d=D))
 
         cos_both = held.tile([D, N], F32, name="cos_both")
         sin_both = held.tile([D, N], F32, name="sin_both")
         for low in (0, HALF):
             nc.scalar.dma_start(cos_both[low : low + HALF], cos_t)
             nc.scalar.dma_start(sin_both[low : low + HALF], sin_t)
-        nc.vector.tensor_scalar_mul(sin_both[0:HALF], sin_both[0:HALF], -1.0)
+
+        identity = held.tile([D, D], F32, name="identity")
+        make_identity(nc, identity[:])
+        rotate = held.tile([D, D], F32, name="rotate")
+        nc.vector.tensor_scalar_mul(rotate[:, 0:HALF], identity[:, HALF:D], -1.0)
+        nc.vector.tensor_copy(rotate[:, HALF:D], identity[:, 0:HALF])
 
         for h in range(H):
             rows = slice(h * D, (h + 1) * D)
             window = cache.tile([D, S], F32, name="window")
             nc.sync.dma_start(window[:], base[rows, :])
 
+            rot = turned.tile([D, N], F32, name="rot")
+            nc.tensor.matmul(rot[:], rotate[:], keys[:, h, :], start=True, stop=True)
+
             by_cos = products.tile([D, N], F32, name="by_cos")
-            nc.vector.tensor_tensor(by_cos[:], k_straight[:, h, :], cos_both[:], MULT)
+            nc.vector.tensor_tensor(by_cos[:], keys[:, h, :], cos_both[:], MULT)
             by_sin = products.tile([D, N], F32, name="by_sin")
-            nc.vector.tensor_tensor(by_sin[:], k_swapped[:, h, :], sin_both[:], MULT)
+            nc.vector.tensor_tensor(by_sin[:], rot[:], sin_both[:], MULT)
 
             nc.vector.tensor_tensor(window[:].indirect(offsets[:]), by_cos[:], by_sin[:], ADD)
             nc.scalar.dma_start(out[rows, :], window[:])

@@ -40,11 +40,14 @@ def tile_lmattention_kernel(tc, base, k_new, cos_t, sin_t, offs, out):
         nc.vector.tensor_scalar_mul(rotate[:, 0:HALF], identity[:, HALF:D], -1.0)
         nc.vector.tensor_copy(rotate[:, HALF:D], identity[:, 0:HALF])
 
+        windows = []
         for h in range(H):
-            rows = slice(h * D, (h + 1) * D)
             window = cache.tile([D, S], F32, name="window")
-            nc.sync.dma_start(window[:], base[rows, :])
+            nc.sync.dma_start(window[:], base[h * D : (h + 1) * D, :])
+            windows.append(window)
 
+        for h in range(H):
+            window = windows[h]
             rot = turned.tile([D, N], F32, name="rot")
             nc.tensor.matmul(rot[:], rotate[:], keys[:, h, :], start=True, stop=True)
 
@@ -54,4 +57,4 @@ def tile_lmattention_kernel(tc, base, k_new, cos_t, sin_t, offs, out):
             nc.vector.tensor_tensor(by_sin[:], rot[:], sin_both[:], MULT)
 
             nc.vector.tensor_tensor(window[:].indirect(offsets[:]), by_cos[:], by_sin[:], ADD)
-            nc.scalar.dma_start(out[rows, :], window[:])
+            nc.sync.dma_start(out[h * D : (h + 1) * D, :], window[:])

@@ -40,10 +40,11 @@ def tile_lmattention_kernel(tc, base, k_new, cos_t, sin_t, offs, out):
         nc.vector.tensor_scalar_mul(rotate[:, 0:HALF], identity[:, HALF:D], -1.0)
         nc.vector.tensor_copy(rotate[:, HALF:D], identity[:, 0:HALF])
 
+        queues = [nc.sync, nc.scalar]
         windows = []
         for h in range(H):
             window = cache.tile([D, S], F32, name="window")
-            nc.sync.dma_start(window[:], base[h * D : (h + 1) * D, :])
+            queues[h % 2].dma_start(window[:], base[h * D : (h + 1) * D, :])
             windows.append(window)
 
         for h in range(H):
@@ -57,4 +58,4 @@ def tile_lmattention_kernel(tc, base, k_new, cos_t, sin_t, offs, out):
             nc.vector.tensor_tensor(by_sin[:], rot[:], sin_both[:], MULT)
 
             nc.vector.tensor_tensor(window[:].indirect(offsets[:]), by_cos[:], by_sin[:], ADD)
-            nc.sync.dma_start(out[h * D : (h + 1) * D, :], window[:])
+            queues[h % 2].dma_start(out[h * D : (h + 1) * D, :], window[:])

@@ -11,6 +11,8 @@ D = 128
 HALF = 64
 S = 1024
 N = 128
+GROUP = 4
+GROUPS = H // GROUP
 
 
 def tile_lmattention_kernel(tc, base, k_new, cos_t, sin_t, offs, out):
@@ -19,8 +21,8 @@ def tile_lmattention_kernel(tc, base, k_new, cos_t, sin_t, offs, out):
     with (
         tc.tile_pool(name="held", bufs=1) as held,
         tc.tile_pool(name="cache", bufs=H) as cache,
-        tc.tile_pool(name="products", bufs=2) as products,
-        tc.psum_pool(name="turned", bufs=2) as turned,
+        tc.tile_pool(name="products", bufs=GROUPS) as products,
+        tc.psum_pool(name="turned", bufs=GROUPS) as turned,
     ):
         offsets = held.tile([D, N // 16], U16, name="offsets")
         nc.sync.dma_start(offsets[:], offs)
@@ -40,22 +42,23 @@ def tile_lmattention_kernel(tc, base, k_new, cos_t, sin_t, offs, out):
         nc.vector.tensor_scalar_mul(rotate[:, 0:HALF], identity[:, HALF:D], -1.0)
         nc.vector.tensor_copy(rotate[:, HALF:D], identity[:, 0:HALF])
 
-        queues = [nc.sync, nc.scalar]
         windows = []
         for h in range(H):
             window = cache.tile([D, S], F32, name="window")
-            queues[h % 2].dma_start(window[:], base[h * D : (h + 1) * D, :])
+            nc.sync.dma_start(window[:], base[h * D : (h + 1) * D, :])
             windows.append(window)
 
-        for h in range(H):
-            window = windows[h]
-            rot = turned.tile([D, N], F32, name="rot")
-            nc.tensor.matmul(rot[:], rotate[:], keys[:, h, :], start=True, stop=True)
+        by_cos = held.tile([D, H, N], F32, name="by_cos")
+        nc.gpsimd.tensor_tensor(by_cos[:], keys[:], cos_both[:].unsqueeze(1).to_broadcast([D, H, N]), MULT)
 
-            by_cos = products.tile([D, N], F32, name="by_cos")
-            nc.vector.tensor_tensor(by_cos[:], keys[:, h, :], cos_both[:], MULT)
-            by_sin = products.tile([D, N], F32, name="by_sin")
-            nc.vector.tensor_tensor(by_sin[:], rot[:], sin_both[:], MULT)
+        for g in range(GROUPS):
+            heads = slice(g * GROUP, (g + 1) * GROUP)
+            rot = turned.tile([D, GROUP, N], F32, name="rot")
+            nc.tensor.matmul(rot[:], rotate[:], keys[:, heads, :], start=True, stop=True)
+            by_sin = products.tile([D, GROUP, N], F32, name="by_sin")
+            nc.vector.tensor_tensor(by_sin[:], rot[:], sin_both[:].unsqueeze(1).to_broadcast([D, GROUP, N]), MULT)
 
-            nc.vector.tensor_tensor(window[:].indirect(offsets[:]), by_cos[:], by_sin[:], ADD)
-            queues[h % 2].dma_start(out[h * D : (h + 1) * D, :], window[:])
+            for i in range(GROUP):
+                h = g * GROUP + i
+                nc.vector.tensor_tensor(windows[h][:].indirect(offsets[:]), by_cos[:, h, :], by_sin[:, i, :], ADD)
+                nc.sync.dma_start(out[h * D : (h + 1) * D, :], windows[h][:])

@@ -23,6 +23,7 @@ def tile_lmattention_kernel(tc, base, k_new, cos_t, sin_t, offs, out):
         tc.tile_pool(name="cache", bufs=H) as cache,
         tc.tile_pool(name="products", bufs=GROUPS) as products,
         tc.psum_pool(name="turned", bufs=GROUPS) as turned,
+        tc.psum_pool(name="spreading", bufs=1) as spreading,
     ):
         offsets = held.tile([D, N // 16], U16, name="offsets")
         nc.sync.dma_start(offsets[:], offs)
@@ -30,17 +31,27 @@ def tile_lmattention_kernel(tc, base, k_new, cos_t, sin_t, offs, out):
         keys = held.tile([D, H, N], F32, name="keys")
         nc.sync.dma_start(keys[:], k_new.rearrange("(h d) j -> d h j", d=D))
 
-        cos_both = held.tile([D, N], F32, name="cos_both")
-        sin_both = held.tile([D, N], F32, name="sin_both")
-        for low in (0, HALF):
-            nc.scalar.dma_start(cos_both[low : low + HALF], cos_t)
-            nc.scalar.dma_start(sin_both[low : low + HALF], sin_t)
+        factors = held.tile([D, N], F32, name="factors")
+        nc.scalar.dma_start(factors[0:HALF], cos_t)
+        nc.scalar.dma_start(factors[HALF:D], sin_t)
 
         identity = held.tile([D, D], F32, name="identity")
         make_identity(nc, identity[:])
         rotate = held.tile([D, D], F32, name="rotate")
         nc.vector.tensor_scalar_mul(rotate[:, 0:HALF], identity[:, HALF:D], -1.0)
         nc.vector.tensor_copy(rotate[:, HALF:D], identity[:, 0:HALF])
+
+        spread_cos = held.tile([D, 2, HALF], F32, name="spread_cos")
+        spread_sin = held.tile([D, 2, HALF], F32, name="spread_sin")
+        nc.vector.tensor_copy(spread_cos[:], identity[:, 0:HALF].unsqueeze(1).to_broadcast([D, 2, HALF]))
+        nc.vector.tensor_copy(spread_sin[:], identity[:, HALF:D].unsqueeze(1).to_broadcast([D, 2, HALF]))
+        spread = spreading.tile([D, 2, N], F32, name="spread")
+        nc.tensor.matmul(spread[:, 0, :], spread_cos[:].rearrange("k t e -> k (t e)"), factors[:], start=True, stop=True)
+        nc.tensor.matmul(spread[:, 1, :], spread_sin[:].rearrange("k t e -> k (t e)"), factors[:], start=True, stop=True)
+        both = held.tile([D, 2, N], F32, name="both")
+        nc.vector.tensor_copy(both[:], spread[:])
+        cos_both = both[:, 0, :]
+        sin_both = both[:, 1, :]
 
         windows = []
         for h in range(H):
@@ -49,14 +60,14 @@ def tile_lmattention_kernel(tc, base, k_new, cos_t, sin_t, offs, out):
             windows.append(window)
 
         by_cos = held.tile([D, H, N], F32, name="by_cos")
-        nc.gpsimd.tensor_tensor(by_cos[:], keys[:], cos_both[:].unsqueeze(1).to_broadcast([D, H, N]), MULT)
+        nc.gpsimd.tensor_tensor(by_cos[:], keys[:], cos_both.unsqueeze(1).to_broadcast([D, H, N]), MULT)
 
         for g in range(GROUPS):
             heads = slice(g * GROUP, (g + 1) * GROUP)
             rot = turned.tile([D, GROUP, N], F32, name="rot")
             nc.tensor.matmul(rot[:], rotate[:], keys[:, heads, :], start=True, stop=True)
             by_sin = products.tile([D, GROUP, N], F32, name="by_sin")
-            nc.vector.tensor_tensor(by_sin[:], rot[:], sin_both[:].unsqueeze(1).to_broadcast([D, GROUP, N]), MULT)
+            nc.vector.tensor_tensor(by_sin[:], rot[:], sin_both.unsqueeze(1).to_broadcast([D, GROUP, N]), MULT)
 
             for i in range(GROUP):
                 h = g * GROUP + i

@@ -6,13 +6,12 @@ U16 = mybir.dt.uint16
 MULT = mybir.AluOpType.mult
 ADD = mybir.AluOpType.add
 
-H = 8
-D = 128
-HALF = 64
+P = 128
 S = 1024
 N = 128
-GROUP = 4
-GROUPS = H // GROUP
+B = 4
+U = 2
+SPAN = 64 // B
 
 
 def tile_lmattention_kernel(tc, base, k_new, cos_t, sin_t, offs, out):
@@ -20,56 +19,60 @@ def tile_lmattention_kernel(tc, base, k_new, cos_t, sin_t, offs, out):
 
     with (
         tc.tile_pool(name="held", bufs=1) as held,
-        tc.tile_pool(name="cache", bufs=H) as cache,
-        tc.tile_pool(name="products", bufs=GROUPS) as products,
-        tc.psum_pool(name="turned", bufs=GROUPS) as turned,
-        tc.psum_pool(name="spreading", bufs=1) as spreading,
+        tc.tile_pool(name="cache", bufs=U * B) as cache,
+        tc.tile_pool(name="products", bufs=2) as products,
+        tc.psum_pool(name="spreading", bufs=2) as spreading,
     ):
-        offsets = held.tile([D, N // 16], U16, name="offsets")
+        offsets = held.tile([P, N // 16], U16, name="offsets")
         nc.sync.dma_start(offsets[:], offs)
 
-        keys = held.tile([D, H, N], F32, name="keys")
-        nc.sync.dma_start(keys[:], k_new.rearrange("(h d) j -> d h j", d=D))
+        factors = held.tile([2 * SPAN, B * N], F32, name="factors")
+        nc.scalar.dma_start(factors[0:SPAN], cos_t.rearrange("(k b) j -> k (b j)", b=B))
+        nc.scalar.dma_start(factors[SPAN : 2 * SPAN], sin_t.rearrange("(k b) j -> k (b j)", b=B))
 
-        factors = held.tile([D, N], F32, name="factors")
-        nc.scalar.dma_start(factors[0:HALF], cos_t)
-        nc.scalar.dma_start(factors[HALF:D], sin_t)
+        keys = held.tile([P, U, B * N], F32, name="keys")
+        nc.sync.dma_start(keys[:], k_new.rearrange("(u p b) j -> p u (b j)", u=U, b=B))
 
-        identity = held.tile([D, D], F32, name="identity")
-        make_identity(nc, identity[:])
-        rotate = held.tile([D, D], F32, name="rotate")
-        nc.vector.tensor_scalar_mul(rotate[:, 0:HALF], identity[:, HALF:D], -1.0)
-        nc.vector.tensor_copy(rotate[:, HALF:D], identity[:, 0:HALF])
-
-        spread_cos = held.tile([D, 2, HALF], F32, name="spread_cos")
-        spread_sin = held.tile([D, 2, HALF], F32, name="spread_sin")
-        nc.vector.tensor_copy(spread_cos[:], identity[:, 0:HALF].unsqueeze(1).to_broadcast([D, 2, HALF]))
-        nc.vector.tensor_copy(spread_sin[:], identity[:, HALF:D].unsqueeze(1).to_broadcast([D, 2, HALF]))
-        spread = spreading.tile([D, 2, N], F32, name="spread")
-        nc.tensor.matmul(spread[:, 0, :], spread_cos[:].rearrange("k t e -> k (t e)"), factors[:], start=True, stop=True)
-        nc.tensor.matmul(spread[:, 1, :], spread_sin[:].rearrange("k t e -> k (t e)"), factors[:], start=True, stop=True)
-        both = held.tile([D, 2, N], F32, name="both")
-        nc.vector.tensor_copy(both[:], spread[:])
-        cos_both = both[:, 0, :]
-        sin_both = both[:, 1, :]
-
+        base_rows = base.rearrange("(u p b) s -> b u p s", u=U, b=B)
+        out_rows = out.rearrange("(u p b) s -> b u p s", u=U, b=B)
         windows = []
-        for h in range(H):
-            window = cache.tile([D, S], F32, name="window")
-            nc.sync.dma_start(window[:], base[h * D : (h + 1) * D, :])
-            windows.append(window)
+        for b in range(B):
+            for u in range(U):
+                window = cache.tile([P, S], F32, name="window")
+                nc.sync.dma_start(window[:], base_rows[b, u])
+                windows.append(window)
 
-        by_cos = held.tile([D, H, N], F32, name="by_cos")
-        nc.gpsimd.tensor_tensor(by_cos[:], keys[:], cos_both.unsqueeze(1).to_broadcast([D, H, N]), MULT)
+        identity = held.tile([P, P], F32, name="identity")
+        make_identity(nc, identity[:])
 
-        for g in range(GROUPS):
-            heads = slice(g * GROUP, (g + 1) * GROUP)
-            rot = turned.tile([D, GROUP, N], F32, name="rot")
-            nc.tensor.matmul(rot[:], rotate[:], keys[:, heads, :], start=True, stop=True)
-            by_sin = products.tile([D, GROUP, N], F32, name="by_sin")
-            nc.vector.tensor_tensor(by_sin[:], rot[:], sin_both.unsqueeze(1).to_broadcast([D, GROUP, N]), MULT)
+        spread_cos = held.tile([2 * SPAN, P // SPAN, SPAN], F32, name="spread_cos")
+        spread_sin = held.tile([2 * SPAN, P // SPAN, SPAN], F32, name="spread_sin")
+        repeated = [2 * SPAN, P // SPAN, SPAN]
+        nc.vector.tensor_copy(spread_cos[:], identity[0 : 2 * SPAN, 0:SPAN].unsqueeze(1).to_broadcast(repeated))
+        nc.vector.tensor_copy(spread_sin[:], identity[0 : 2 * SPAN, SPAN : 2 * SPAN].unsqueeze(1).to_broadcast(repeated))
 
-            for i in range(GROUP):
-                h = g * GROUP + i
-                nc.vector.tensor_tensor(windows[h][:].indirect(offsets[:]), by_cos[:, h, :], by_sin[:, i, :], ADD)
-                nc.sync.dma_start(out[h * D : (h + 1) * D, :], windows[h][:])
+        rotate = held.tile([P, P // (2 * SPAN), 2, SPAN], F32, name="rotate")
+        halves = identity[:].rearrange("k (g t e) -> k g t e", t=2, e=SPAN)
+        nc.vector.tensor_scalar_mul(rotate[:, :, 0, :], halves[:, :, 1, :], -1.0)
+        nc.vector.tensor_copy(rotate[:, :, 1, :], halves[:, :, 0, :])
+
+        for b in range(B):
+            tokens = slice(b * N, (b + 1) * N)
+            cos_spread = spreading.tile([P, N], F32, name="cos_spread")
+            sin_spread = spreading.tile([P, N], F32, name="sin_spread")
+            rot = spreading.tile([P, U, N], F32, name="rot")
+            nc.tensor.matmul(cos_spread[:], spread_cos[:].rearrange("k g e -> k (g e)"), factors[:, tokens], start=True, stop=True)
+            nc.tensor.matmul(sin_spread[:], spread_sin[:].rearrange("k g e -> k (g e)"), factors[:, tokens], start=True, stop=True)
+            nc.tensor.matmul(rot[:], rotate[:].rearrange("k g t e -> k (g t e)"), keys[:, :, tokens], start=True, stop=True)
+
+            sin_here = products.tile([P, N], F32, name="sin_here")
+            nc.scalar.copy(sin_here[:], sin_spread[:])
+            by_cos = products.tile([P, U, N], F32, name="by_cos")
+            by_sin = products.tile([P, U, N], F32, name="by_sin")
+            nc.vector.tensor_tensor(by_cos[:], keys[:, :, tokens], cos_spread[:].unsqueeze(1).to_broadcast([P, U, N]), MULT)
+            nc.vector.tensor_tensor(by_sin[:], rot[:], sin_here[:].unsqueeze(1).to_broadcast([P, U, N]), MULT)
+
+            for u in range(U):
+                window = windows[b * U + u]
+                nc.vector.tensor_tensor(window[:].indirect(offsets[:]), by_cos[:, u, :], by_sin[:, u, :], ADD)
+                nc.sync.dma_start(out_rows[b, u], window[:])

@@ -12,6 +12,7 @@ N = 128
 B = 4
 U = 2
 SPAN = 64 // B
+PAIR = 2
 
 
 def tile_lmattention_kernel(tc, base, k_new, cos_t, sin_t, offs, out):
@@ -21,6 +22,7 @@ def tile_lmattention_kernel(tc, base, k_new, cos_t, sin_t, offs, out):
         tc.tile_pool(name="held", bufs=1) as held,
         tc.tile_pool(name="cache", bufs=U * B) as cache,
         tc.tile_pool(name="products", bufs=2) as products,
+        tc.tile_pool(name="arriving", bufs=U * B // PAIR) as arriving,
         tc.psum_pool(name="spreading", bufs=2) as spreading,
     ):
         offsets = held.tile([P, N // 16], U16, name="offsets")
@@ -33,14 +35,13 @@ def tile_lmattention_kernel(tc, base, k_new, cos_t, sin_t, offs, out):
         keys = held.tile([P, U, B * N], F32, name="keys")
         nc.sync.dma_start(keys[:], k_new.rearrange("(u p b) j -> p u (b j)", u=U, b=B))
 
-        base_rows = base.rearrange("(u p b) s -> b u p s", u=U, b=B)
+        base_pairs = base.rearrange("(u p c b) s -> c u p (b s)", u=U, c=B // PAIR, b=PAIR)
         out_rows = out.rearrange("(u p b) s -> b u p s", u=U, b=B)
-        windows = []
-        for b in range(B):
+        pairs = {}
+        for c in range(B // PAIR):
             for u in range(U):
-                window = cache.tile([P, S], F32, name="window")
-                nc.sync.dma_start(window[:], base_rows[b, u])
-                windows.append(window)
+                pairs[c, u] = arriving.tile([P, PAIR, S], F32, name="pair")
+                nc.sync.dma_start(pairs[c, u][:].rearrange("p b s -> p (b s)"), base_pairs[c, u])
 
         identity = held.tile([P, P], F32, name="identity")
         make_identity(nc, identity[:])
@@ -73,6 +74,7 @@ def tile_lmattention_kernel(tc, base, k_new, cos_t, sin_t, offs, out):
             nc.vector.tensor_tensor(by_sin[:], rot[:], sin_here[:].unsqueeze(1).to_broadcast([P, U, N]), MULT)
 
             for u in range(U):
-                window = windows[b * U + u]
+                window = cache.tile([P, S], F32, name="window")
+                nc.scalar.copy(window[:], pairs[b // PAIR, u][:, b % PAIR, :])
                 nc.vector.tensor_tensor(window[:].indirect(offsets[:]), by_cos[:, u, :], by_sin[:, u, :], ADD)
                 nc.sync.dma_start(out_rows[b, u], window[:])

@@ -9,10 +9,9 @@ ADD = mybir.AluOpType.add
 P = 128
 S = 1024
 N = 128
-B = 4
-U = 2
+B = 2
+U = 4
 SPAN = 64 // B
-PAIR = 2
 
 
 def tile_lmattention_kernel(tc, base, k_new, cos_t, sin_t, offs, out):
@@ -20,61 +19,59 @@ def tile_lmattention_kernel(tc, base, k_new, cos_t, sin_t, offs, out):
 
     with (
         tc.tile_pool(name="held", bufs=1) as held,
+        tc.tile_pool(name="arriving", bufs=U) as arriving,
         tc.tile_pool(name="cache", bufs=U * B) as cache,
         tc.tile_pool(name="products", bufs=2) as products,
-        tc.tile_pool(name="arriving", bufs=U * B // PAIR) as arriving,
-        tc.psum_pool(name="spreading", bufs=2) as spreading,
+        tc.psum_pool(name="spreading", bufs=1) as spreading,
+        tc.psum_pool(name="turned", bufs=2) as turned,
     ):
+        cos_rows = held.tile([SPAN, B * N], F32, name="cos_rows")
+        sin_rows = held.tile([SPAN, B * N], F32, name="sin_rows")
+        nc.sync.dma_start(cos_rows[:], cos_t.rearrange("(k b) j -> k (b j)", b=B))
+        nc.sync.dma_start(sin_rows[:], sin_t.rearrange("(k b) j -> k (b j)", b=B))
+
         offsets = held.tile([P, N // 16], U16, name="offsets")
         nc.sync.dma_start(offsets[:], offs)
-
-        factors = held.tile([2 * SPAN, B * N], F32, name="factors")
-        nc.scalar.dma_start(factors[0:SPAN], cos_t.rearrange("(k b) j -> k (b j)", b=B))
-        nc.scalar.dma_start(factors[SPAN : 2 * SPAN], sin_t.rearrange("(k b) j -> k (b j)", b=B))
 
         keys = held.tile([P, U, B * N], F32, name="keys")
         nc.sync.dma_start(keys[:], k_new.rearrange("(u p b) j -> p u (b j)", u=U, b=B))
 
-        base_pairs = base.rearrange("(u p c b) s -> c u p (b s)", u=U, c=B // PAIR, b=PAIR)
-        out_rows = out.rearrange("(u p b) s -> b u p s", u=U, b=B)
-        pairs = {}
-        for c in range(B // PAIR):
-            for u in range(U):
-                pairs[c, u] = arriving.tile([P, PAIR, S], F32, name="pair")
-                nc.sync.dma_start(pairs[c, u][:].rearrange("p b s -> p (b s)"), base_pairs[c, u])
+        blocks = []
+        for u in range(U):
+            block = arriving.tile([P, B, S], F32, name="block")
+            nc.sync.dma_start(block[:].rearrange("p b s -> p (b s)"), base.rearrange("(u p b) s -> u p (b s)", u=U, b=B)[u])
+            blocks.append(block)
+        out_rows = out.rearrange("(u p b) s -> u b p s", u=U, b=B)
 
         identity = held.tile([P, P], F32, name="identity")
         make_identity(nc, identity[:])
-
-        spread_cos = held.tile([2 * SPAN, P // SPAN, SPAN], F32, name="spread_cos")
-        spread_sin = held.tile([2 * SPAN, P // SPAN, SPAN], F32, name="spread_sin")
-        repeated = [2 * SPAN, P // SPAN, SPAN]
-        nc.vector.tensor_copy(spread_cos[:], identity[0 : 2 * SPAN, 0:SPAN].unsqueeze(1).to_broadcast(repeated))
-        nc.vector.tensor_copy(spread_sin[:], identity[0 : 2 * SPAN, SPAN : 2 * SPAN].unsqueeze(1).to_broadcast(repeated))
 
         rotate = held.tile([P, P // (2 * SPAN), 2, SPAN], F32, name="rotate")
         halves = identity[:].rearrange("k (g t e) -> k g t e", t=2, e=SPAN)
         nc.vector.tensor_scalar_mul(rotate[:, :, 0, :], halves[:, :, 1, :], -1.0)
         nc.vector.tensor_copy(rotate[:, :, 1, :], halves[:, :, 0, :])
 
-        for b in range(B):
-            tokens = slice(b * N, (b + 1) * N)
-            cos_spread = spreading.tile([P, N], F32, name="cos_spread")
-            sin_spread = spreading.tile([P, N], F32, name="sin_spread")
-            rot = spreading.tile([P, U, N], F32, name="rot")
-            nc.tensor.matmul(cos_spread[:], spread_cos[:].rearrange("k g e -> k (g e)"), factors[:, tokens], start=True, stop=True)
-            nc.tensor.matmul(sin_spread[:], spread_sin[:].rearrange("k g e -> k (g e)"), factors[:, tokens], start=True, stop=True)
-            nc.tensor.matmul(rot[:], rotate[:].rearrange("k g t e -> k (g t e)"), keys[:, :, tokens], start=True, stop=True)
+        spread = held.tile([SPAN, P // SPAN, SPAN], F32, name="spread")
+        nc.vector.tensor_copy(spread[:], identity[0:SPAN, 0:SPAN].unsqueeze(1).to_broadcast([SPAN, P // SPAN, SPAN]))
+        cos_spread = spreading.tile([P, B * N], F32, name="cos_spread")
+        sin_spread = spreading.tile([P, B * N], F32, name="sin_spread")
+        nc.tensor.matmul(cos_spread[:], spread[:].rearrange("k g e -> k (g e)"), cos_rows[:], start=True, stop=True)
+        nc.tensor.matmul(sin_spread[:], spread[:].rearrange("k g e -> k (g e)"), sin_rows[:], start=True, stop=True)
 
-            sin_here = products.tile([P, N], F32, name="sin_here")
-            nc.scalar.copy(sin_here[:], sin_spread[:])
-            by_cos = products.tile([P, U, N], F32, name="by_cos")
-            by_sin = products.tile([P, U, N], F32, name="by_sin")
-            nc.vector.tensor_tensor(by_cos[:], keys[:, :, tokens], cos_spread[:].unsqueeze(1).to_broadcast([P, U, N]), MULT)
-            nc.vector.tensor_tensor(by_sin[:], rot[:], sin_here[:].unsqueeze(1).to_broadcast([P, U, N]), MULT)
+        sin_all = held.tile([P, B * N], F32, name="sin_all")
+        nc.scalar.copy(sin_all[:], sin_spread[:])
+        by_cos = held.tile([P, U, B * N], F32, name="by_cos")
+        nc.vector.tensor_tensor(by_cos[:], keys[:], cos_spread[:].unsqueeze(1).to_broadcast([P, U, B * N]), MULT)
 
-            for u in range(U):
+        for u in range(U):
+            rot = turned.tile([P, B * N], F32, name="rot")
+            nc.tensor.matmul(rot[:], rotate[:].rearrange("k g t e -> k (g t e)"), keys[:, u, :], start=True, stop=True)
+            by_sin = products.tile([P, B * N], F32, name="by_sin")
+            nc.vector.tensor_tensor(by_sin[:], rot[:], sin_all[:], MULT)
+
+            for b in range(B):
+                tokens = slice(b * N, (b + 1) * N)
                 window = cache.tile([P, S], F32, name="window")
-                nc.scalar.copy(window[:], pairs[b // PAIR, u][:, b % PAIR, :])
-                nc.vector.tensor_tensor(window[:].indirect(offsets[:]), by_cos[:, u, :], by_sin[:, u, :], ADD)
-                nc.sync.dma_start(out_rows[b, u], window[:])
+                nc.scalar.copy(window[:], blocks[u][:, b, :])
+                nc.vector.tensor_tensor(window[:].indirect(offsets[:]), by_cos[:, u, tokens], by_sin[:, tokens], ADD)
+                nc.sync.dma_start(out_rows[u, b], window[:])

@@ -9,9 +9,10 @@ ADD = mybir.AluOpType.add
 P = 128
 S = 1024
 N = 128
+U = 2
+C = 2
 B = 2
-U = 4
-SPAN = 64 // B
+SPAN = 64 // (C * B)
 
 
 def tile_lmattention_kernel(tc, base, k_new, cos_t, sin_t, offs, out):
@@ -19,29 +20,29 @@ def tile_lmattention_kernel(tc, base, k_new, cos_t, sin_t, offs, out):
 
     with (
         tc.tile_pool(name="held", bufs=1) as held,
-        tc.tile_pool(name="arriving", bufs=U) as arriving,
-        tc.tile_pool(name="cache", bufs=U * B) as cache,
+        tc.tile_pool(name="arriving", bufs=U * C) as arriving,
+        tc.tile_pool(name="cache", bufs=U * C * B) as cache,
         tc.tile_pool(name="products", bufs=2) as products,
-        tc.psum_pool(name="spreading", bufs=1) as spreading,
+        tc.psum_pool(name="spreading", bufs=2) as spreading,
         tc.psum_pool(name="turned", bufs=2) as turned,
     ):
-        cos_rows = held.tile([SPAN, B * N], F32, name="cos_rows")
-        sin_rows = held.tile([SPAN, B * N], F32, name="sin_rows")
-        nc.sync.dma_start(cos_rows[:], cos_t.rearrange("(k b) j -> k (b j)", b=B))
-        nc.sync.dma_start(sin_rows[:], sin_t.rearrange("(k b) j -> k (b j)", b=B))
+        factors = held.tile([2 * SPAN, C, B * N], F32, name="factors")
+        nc.sync.dma_start(factors[0:SPAN].rearrange("k c f -> k (c f)"), cos_t.rearrange("(k r) j -> k (r j)", r=C * B))
+        nc.sync.dma_start(factors[SPAN : 2 * SPAN].rearrange("k c f -> k (c f)"), sin_t.rearrange("(k r) j -> k (r j)", r=C * B))
 
         offsets = held.tile([P, N // 16], U16, name="offsets")
         nc.sync.dma_start(offsets[:], offs)
 
-        keys = held.tile([P, U, B * N], F32, name="keys")
-        nc.sync.dma_start(keys[:], k_new.rearrange("(u p b) j -> p u (b j)", u=U, b=B))
+        keys = held.tile([P, U, C, B * N], F32, name="keys")
+        nc.sync.dma_start(keys[:].rearrange("p u c f -> p u (c f)"), k_new.rearrange("(u p r) j -> p u (r j)", u=U, r=C * B))
 
-        blocks = []
-        for u in range(U):
-            block = arriving.tile([P, B, S], F32, name="block")
-            nc.sync.dma_start(block[:].rearrange("p b s -> p (b s)"), base.rearrange("(u p b) s -> u p (b s)", u=U, b=B)[u])
-            blocks.append(block)
-        out_rows = out.rearrange("(u p b) s -> u b p s", u=U, b=B)
+        base_pairs = base.rearrange("(u p c b) s -> c u p (b s)", u=U, c=C, b=B)
+        out_rows = out.rearrange("(u p c b) s -> c u b p s", u=U, c=C, b=B)
+        pairs = {}
+        for c in range(C):
+            for u in range(U):
+                pairs[c, u] = arriving.tile([P, B, S], F32, name="pair")
+                nc.sync.dma_start(pairs[c, u][:].rearrange("p b s -> p (b s)"), base_pairs[c, u])
 
         identity = held.tile([P, P], F32, name="identity")
         make_identity(nc, identity[:])
@@ -51,27 +52,32 @@ def tile_lmattention_kernel(tc, base, k_new, cos_t, sin_t, offs, out):
         nc.vector.tensor_scalar_mul(rotate[:, :, 0, :], halves[:, :, 1, :], -1.0)
         nc.vector.tensor_copy(rotate[:, :, 1, :], halves[:, :, 0, :])
 
-        spread = held.tile([SPAN, P // SPAN, SPAN], F32, name="spread")
-        nc.vector.tensor_copy(spread[:], identity[0:SPAN, 0:SPAN].unsqueeze(1).to_broadcast([SPAN, P // SPAN, SPAN]))
-        cos_spread = spreading.tile([P, B * N], F32, name="cos_spread")
-        sin_spread = spreading.tile([P, B * N], F32, name="sin_spread")
-        nc.tensor.matmul(cos_spread[:], spread[:].rearrange("k g e -> k (g e)"), cos_rows[:], start=True, stop=True)
-        nc.tensor.matmul(sin_spread[:], spread[:].rearrange("k g e -> k (g e)"), sin_rows[:], start=True, stop=True)
+        spread_cos = held.tile([2 * SPAN, P // SPAN, SPAN], F32, name="spread_cos")
+        spread_sin = held.tile([2 * SPAN, P // SPAN, SPAN], F32, name="spread_sin")
+        repeated = [2 * SPAN, P // SPAN, SPAN]
+        nc.vector.tensor_copy(spread_cos[:], identity[0 : 2 * SPAN, 0:SPAN].unsqueeze(1).to_broadcast(repeated))
+        nc.vector.tensor_copy(spread_sin[:], identity[0 : 2 * SPAN, SPAN : 2 * SPAN].unsqueeze(1).to_broadcast(repeated))
 
-        sin_all = held.tile([P, B * N], F32, name="sin_all")
-        nc.scalar.copy(sin_all[:], sin_spread[:])
-        by_cos = held.tile([P, U, B * N], F32, name="by_cos")
-        nc.vector.tensor_tensor(by_cos[:], keys[:], cos_spread[:].unsqueeze(1).to_broadcast([P, U, B * N]), MULT)
+        for c in range(C):
+            cos_spread = spreading.tile([P, B * N], F32, name="cos_spread")
+            sin_spread = spreading.tile([P, B * N], F32, name="sin_spread")
+            nc.tensor.matmul(cos_spread[:], spread_cos[:].rearrange("k g e -> k (g e)"), factors[:, c, :], start=True, stop=True)
+            nc.tensor.matmul(sin_spread[:], spread_sin[:].rearrange("k g e -> k (g e)"), factors[:, c, :], start=True, stop=True)
 
-        for u in range(U):
-            rot = turned.tile([P, B * N], F32, name="rot")
-            nc.tensor.matmul(rot[:], rotate[:].rearrange("k g t e -> k (g t e)"), keys[:, u, :], start=True, stop=True)
-            by_sin = products.tile([P, B * N], F32, name="by_sin")
-            nc.vector.tensor_tensor(by_sin[:], rot[:], sin_all[:], MULT)
+            sin_here = products.tile([P, B * N], F32, name="sin_here")
+            nc.scalar.copy(sin_here[:], sin_spread[:])
+            by_cos = products.tile([P, U, B * N], F32, name="by_cos")
+            nc.vector.tensor_tensor(by_cos[:], keys[:, :, c, :], cos_spread[:].unsqueeze(1).to_broadcast([P, U, B * N]), MULT)
 
-            for b in range(B):
-                tokens = slice(b * N, (b + 1) * N)
-                window = cache.tile([P, S], F32, name="window")
-                nc.scalar.copy(window[:], blocks[u][:, b, :])
-                nc.vector.tensor_tensor(window[:].indirect(offsets[:]), by_cos[:, u, tokens], by_sin[:, tokens], ADD)
-                nc.sync.dma_start(out_rows[u, b], window[:])
+            for u in range(U):
+                rot = turned.tile([P, B * N], F32, name="rot")
+                nc.tensor.matmul(rot[:], rotate[:].rearrange("k g t e -> k (g t e)"), keys[:, u, c, :], start=True, stop=True)
+                by_sin = products.tile([P, B * N], F32, name="by_sin")
+                nc.vector.tensor_tensor(by_sin[:], rot[:], sin_here[:], MULT)
+
+                for b in range(B):
+                    tokens = slice(b * N, (b + 1) * N)
+                    window = cache.tile([P, S], F32, name="window")
+                    nc.scalar.copy(window[:], pairs[c, u][:, b, :])
+                    nc.vector.tensor_tensor(window[:].indirect(offsets[:]), by_cos[:, u, tokens], by_sin[:, tokens], ADD)
+                    nc.sync.dma_start(out_rows[c, u, b], window[:])

@@ -9,10 +9,14 @@ ADD = mybir.AluOpType.add
 P = 128
 S = 1024
 N = 128
-U = 2
-C = 2
+R = 8
 B = 2
-SPAN = 64 // (C * B)
+C = R // B
+SPAN = 64 // R
+F = 4
+HELD_ON = 64 // F
+
+LOADS = [2, 3, 3]
 
 
 def tile_lmattention_kernel(tc, base, k_new, cos_t, sin_t, offs, out):
@@ -20,64 +24,65 @@ def tile_lmattention_kernel(tc, base, k_new, cos_t, sin_t, offs, out):
 
     with (
         tc.tile_pool(name="held", bufs=1) as held,
-        tc.tile_pool(name="arriving", bufs=U * C) as arriving,
-        tc.tile_pool(name="cache", bufs=U * C * B) as cache,
+        tc.tile_pool(name="cache", bufs=R) as cache,
         tc.tile_pool(name="products", bufs=2) as products,
         tc.psum_pool(name="spreading", bufs=2) as spreading,
         tc.psum_pool(name="turned", bufs=2) as turned,
     ):
-        factors = held.tile([2 * SPAN, C, B * N], F32, name="factors")
-        nc.sync.dma_start(factors[0:SPAN].rearrange("k c f -> k (c f)"), cos_t.rearrange("(k r) j -> k (r j)", r=C * B))
-        nc.sync.dma_start(factors[SPAN : 2 * SPAN].rearrange("k c f -> k (c f)"), sin_t.rearrange("(k r) j -> k (r j)", r=C * B))
+        factors = held.tile([2 * HELD_ON, F // B, B * N], F32, name="factors")
+        nc.sync.dma_start(factors[0:HELD_ON].rearrange("k c f -> k (c f)"), cos_t.rearrange("(k i) j -> k (i j)", i=F))
+        nc.sync.dma_start(factors[HELD_ON : 2 * HELD_ON].rearrange("k c f -> k (c f)"), sin_t.rearrange("(k i) j -> k (i j)", i=F))
 
         offsets = held.tile([P, N // 16], U16, name="offsets")
         nc.sync.dma_start(offsets[:], offs)
 
-        keys = held.tile([P, U, C, B * N], F32, name="keys")
-        nc.sync.dma_start(keys[:].rearrange("p u c f -> p u (c f)"), k_new.rearrange("(u p r) j -> p u (r j)", u=U, r=C * B))
+        keys = held.tile([P, C, B * N], F32, name="keys")
+        nc.sync.dma_start(keys[:].rearrange("p c f -> p (c f)"), k_new.rearrange("(p i) j -> p (i j)", i=R))
 
-        base_pairs = base.rearrange("(u p c b) s -> c u p (b s)", u=U, c=C, b=B)
-        out_rows = out.rearrange("(u p c b) s -> c u b p s", u=U, c=C, b=B)
-        pairs = {}
-        for c in range(C):
-            for u in range(U):
-                pairs[c, u] = arriving.tile([P, B, S], F32, name="pair")
-                nc.sync.dma_start(pairs[c, u][:].rearrange("p b s -> p (b s)"), base_pairs[c, u])
+        base_rows = base.rearrange("(p i) s -> p i s", i=R)
+        out_rows = out.rearrange("(p i) s -> p i s", i=R)
+        row_arrives_in = []
+        for count in LOADS:
+            first = len(row_arrives_in)
+            arrived = held.tile([P, count, S], F32, name=f"arrived_{first}")
+            nc.sync.dma_start(arrived[:], base_rows[:, first : first + count, :])
+            row_arrives_in += [arrived[:, k, :] for k in range(count)]
 
         identity = held.tile([P, P], F32, name="identity")
         make_identity(nc, identity[:])
+
+        picks = identity[0 : 2 * HELD_ON, 0 : 2 * HELD_ON].rearrange("k (t e h) -> k t h e", t=2, h=R // F)
+        spread = held.tile([2 * HELD_ON, 2, R // F, P // SPAN, SPAN], F32, name="spread")
+        for half in range(R // F):
+            for table in range(2):
+                repeated = [2 * HELD_ON, P // SPAN, SPAN]
+                nc.vector.tensor_copy(spread[:, table, half], picks[:, table, half, :].unsqueeze(1).to_broadcast(repeated))
 
         rotate = held.tile([P, P // (2 * SPAN), 2, SPAN], F32, name="rotate")
         halves = identity[:].rearrange("k (g t e) -> k g t e", t=2, e=SPAN)
         nc.vector.tensor_scalar_mul(rotate[:, :, 0, :], halves[:, :, 1, :], -1.0)
         nc.vector.tensor_copy(rotate[:, :, 1, :], halves[:, :, 0, :])
 
-        spread_cos = held.tile([2 * SPAN, P // SPAN, SPAN], F32, name="spread_cos")
-        spread_sin = held.tile([2 * SPAN, P // SPAN, SPAN], F32, name="spread_sin")
-        repeated = [2 * SPAN, P // SPAN, SPAN]
-        nc.vector.tensor_copy(spread_cos[:], identity[0 : 2 * SPAN, 0:SPAN].unsqueeze(1).to_broadcast(repeated))
-        nc.vector.tensor_copy(spread_sin[:], identity[0 : 2 * SPAN, SPAN : 2 * SPAN].unsqueeze(1).to_broadcast(repeated))
-
         for c in range(C):
+            half, part = divmod(c, F // B)
             cos_spread = spreading.tile([P, B * N], F32, name="cos_spread")
             sin_spread = spreading.tile([P, B * N], F32, name="sin_spread")
-            nc.tensor.matmul(cos_spread[:], spread_cos[:].rearrange("k g e -> k (g e)"), factors[:, c, :], start=True, stop=True)
-            nc.tensor.matmul(sin_spread[:], spread_sin[:].rearrange("k g e -> k (g e)"), factors[:, c, :], start=True, stop=True)
+            rot = turned.tile([P, B * N], F32, name="rot")
+            nc.tensor.matmul(cos_spread[:], spread[:, 0, half].rearrange("k g e -> k (g e)"), factors[:, part, :], start=True, stop=True)
+            nc.tensor.matmul(sin_spread[:], spread[:, 1, half].rearrange("k g e -> k (g e)"), factors[:, part, :], start=True, stop=True)
+            nc.tensor.matmul(rot[:], rotate[:].rearrange("k g t e -> k (g t e)"), keys[:, c, :], start=True, stop=True)
 
             sin_here = products.tile([P, B * N], F32, name="sin_here")
             nc.scalar.copy(sin_here[:], sin_spread[:])
-            by_cos = products.tile([P, U, B * N], F32, name="by_cos")
-            nc.vector.tensor_tensor(by_cos[:], keys[:, :, c, :], cos_spread[:].unsqueeze(1).to_broadcast([P, U, B * N]), MULT)
+            by_cos = products.tile([P, B * N], F32, name="by_cos")
+            nc.vector.tensor_tensor(by_cos[:], keys[:, c, :], cos_spread[:], MULT)
+            by_sin = products.tile([P, B * N], F32, name="by_sin")
+            nc.vector.tensor_tensor(by_sin[:], rot[:], sin_here[:], MULT)
 
-            for u in range(U):
-                rot = turned.tile([P, B * N], F32, name="rot")
-                nc.tensor.matmul(rot[:], rotate[:].rearrange("k g t e -> k (g t e)"), keys[:, u, c, :], start=True, stop=True)
-                by_sin = products.tile([P, B * N], F32, name="by_sin")
-                nc.vector.tensor_tensor(by_sin[:], rot[:], sin_here[:], MULT)
-
-                for b in range(B):
-                    tokens = slice(b * N, (b + 1) * N)
-                    window = cache.tile([P, S], F32, name="window")
-                    nc.scalar.copy(window[:], pairs[c, u][:, b, :])
-                    nc.vector.tensor_tensor(window[:].indirect(offsets[:]), by_cos[:, u, tokens], by_sin[:, tokens], ADD)
-                    nc.sync.dma_start(out_rows[c, u, b], window[:])
+            for b in range(B):
+                i = c * B + b
+                tokens = slice(b * N, (b + 1) * N)
+                window = cache.tile([P, S], F32, name="window")
+                nc.scalar.copy(window[:], row_arrives_in[i])
+                nc.vector.tensor_tensor(window[:].indirect(offsets[:]), by_cos[:, tokens], by_sin[:, tokens], ADD)
+                nc.sync.dma_start(out_rows[:, i, :], window[:])

@@ -9,14 +9,10 @@ ADD = mybir.AluOpType.add
 P = 128
 S = 1024
 N = 128
-R = 8
+U = 2
+C = 2
 B = 2
-C = R // B
-SPAN = 64 // R
-F = 4
-HELD_ON = 64 // F
-
-LOADS = [2, 3, 3]
+SPAN = 64 // (C * B)
 
 
 def tile_lmattention_kernel(tc, base, k_new, cos_t, sin_t, offs, out):
@@ -24,65 +20,70 @@ def tile_lmattention_kernel(tc, base, k_new, cos_t, sin_t, offs, out):
 
     with (
         tc.tile_pool(name="held", bufs=1) as held,
-        tc.tile_pool(name="cache", bufs=R) as cache,
-        tc.tile_pool(name="products", bufs=2) as products,
-        tc.psum_pool(name="spreading", bufs=2) as spreading,
-        tc.psum_pool(name="turned", bufs=2) as turned,
+        tc.tile_pool(name="cache", bufs=U * C * B) as cache,
+        tc.tile_pool(name="products", bufs=C) as products,
+        tc.psum_pool(name="spreading", bufs=C) as spreading,
+        tc.psum_pool(name="turned", bufs=C) as turned,
     ):
-        factors = held.tile([2 * HELD_ON, F // B, B * N], F32, name="factors")
-        nc.sync.dma_start(factors[0:HELD_ON].rearrange("k c f -> k (c f)"), cos_t.rearrange("(k i) j -> k (i j)", i=F))
-        nc.sync.dma_start(factors[HELD_ON : 2 * HELD_ON].rearrange("k c f -> k (c f)"), sin_t.rearrange("(k i) j -> k (i j)", i=F))
+        factors = held.tile([2 * SPAN, C, B * N], F32, name="factors")
+        nc.sync.dma_start(factors[0:SPAN].rearrange("k c f -> k (c f)"), cos_t.rearrange("(k r) j -> k (r j)", r=C * B))
+        nc.sync.dma_start(factors[SPAN : 2 * SPAN].rearrange("k c f -> k (c f)"), sin_t.rearrange("(k r) j -> k (r j)", r=C * B))
 
         offsets = held.tile([P, N // 16], U16, name="offsets")
         nc.sync.dma_start(offsets[:], offs)
 
-        keys = held.tile([P, C, B * N], F32, name="keys")
-        nc.sync.dma_start(keys[:].rearrange("p c f -> p (c f)"), k_new.rearrange("(p i) j -> p (i j)", i=R))
+        keys = held.tile([P, U, C, B * N], F32, name="keys")
+        nc.sync.dma_start(keys[:].rearrange("p u c f -> p u (c f)"), k_new.rearrange("(u p r) j -> p u (r j)", u=U, r=C * B))
 
-        base_rows = base.rearrange("(p i) s -> p i s", i=R)
-        out_rows = out.rearrange("(p i) s -> p i s", i=R)
-        row_arrives_in = []
-        for count in LOADS:
-            first = len(row_arrives_in)
-            arrived = held.tile([P, count, S], F32, name=f"arrived_{first}")
-            nc.sync.dma_start(arrived[:], base_rows[:, first : first + count, :])
-            row_arrives_in += [arrived[:, k, :] for k in range(count)]
+        base_rows = base.rearrange("(u p r) s -> u p r s", u=U, r=C * B)
+        out_rows = out.rearrange("(u p r) s -> u r p s", u=U, r=C * B)
+        arrived = {}
+        for c in range(C):
+            pair = held.tile([P, B, S], F32, name=f"pair_{c}")
+            nc.sync.dma_start(pair[:], base_rows[0, :, c * B : (c + 1) * B, :])
+            for b in range(B):
+                arrived[0, c, b] = pair[:, b, :]
+        four = held.tile([P, C, B, S], F32, name="four")
+        nc.sync.dma_start(four[:].rearrange("p c b s -> p (c b) s"), base_rows[1])
+        for c in range(C):
+            for b in range(B):
+                arrived[1, c, b] = four[:, c, b, :]
 
         identity = held.tile([P, P], F32, name="identity")
         make_identity(nc, identity[:])
 
-        picks = identity[0 : 2 * HELD_ON, 0 : 2 * HELD_ON].rearrange("k (t e h) -> k t h e", t=2, h=R // F)
-        spread = held.tile([2 * HELD_ON, 2, R // F, P // SPAN, SPAN], F32, name="spread")
-        for half in range(R // F):
-            for table in range(2):
-                repeated = [2 * HELD_ON, P // SPAN, SPAN]
-                nc.vector.tensor_copy(spread[:, table, half], picks[:, table, half, :].unsqueeze(1).to_broadcast(repeated))
+        spread_cos = held.tile([2 * SPAN, P // SPAN, SPAN], F32, name="spread_cos")
+        spread_sin = held.tile([2 * SPAN, P // SPAN, SPAN], F32, name="spread_sin")
+        repeated = [2 * SPAN, P // SPAN, SPAN]
+        nc.vector.tensor_copy(spread_cos[:], identity[0 : 2 * SPAN, 0:SPAN].unsqueeze(1).to_broadcast(repeated))
+        nc.vector.tensor_copy(spread_sin[:], identity[0 : 2 * SPAN, SPAN : 2 * SPAN].unsqueeze(1).to_broadcast(repeated))
 
         rotate = held.tile([P, P // (2 * SPAN), 2, SPAN], F32, name="rotate")
         halves = identity[:].rearrange("k (g t e) -> k g t e", t=2, e=SPAN)
         nc.vector.tensor_scalar_mul(rotate[:, :, 0, :], halves[:, :, 1, :], -1.0)
         nc.vector.tensor_copy(rotate[:, :, 1, :], halves[:, :, 0, :])
 
+        cosines, sines = [], []
         for c in range(C):
-            half, part = divmod(c, F // B)
             cos_spread = spreading.tile([P, B * N], F32, name="cos_spread")
             sin_spread = spreading.tile([P, B * N], F32, name="sin_spread")
-            rot = turned.tile([P, B * N], F32, name="rot")
-            nc.tensor.matmul(cos_spread[:], spread[:, 0, half].rearrange("k g e -> k (g e)"), factors[:, part, :], start=True, stop=True)
-            nc.tensor.matmul(sin_spread[:], spread[:, 1, half].rearrange("k g e -> k (g e)"), factors[:, part, :], start=True, stop=True)
-            nc.tensor.matmul(rot[:], rotate[:].rearrange("k g t e -> k (g t e)"), keys[:, c, :], start=True, stop=True)
-
+            nc.tensor.matmul(cos_spread[:], spread_cos[:].rearrange("k g e -> k (g e)"), factors[:, c, :], start=True, stop=True)
+            nc.tensor.matmul(sin_spread[:], spread_sin[:].rearrange("k g e -> k (g e)"), factors[:, c, :], start=True, stop=True)
             sin_here = products.tile([P, B * N], F32, name="sin_here")
             nc.scalar.copy(sin_here[:], sin_spread[:])
-            by_cos = products.tile([P, B * N], F32, name="by_cos")
-            nc.vector.tensor_tensor(by_cos[:], keys[:, c, :], cos_spread[:], MULT)
-            by_sin = products.tile([P, B * N], F32, name="by_sin")
-            nc.vector.tensor_tensor(by_sin[:], rot[:], sin_here[:], MULT)
+            cosines.append(cos_spread)
+            sines.append(sin_here)
 
-            for b in range(B):
-                i = c * B + b
-                tokens = slice(b * N, (b + 1) * N)
-                window = cache.tile([P, S], F32, name="window")
-                nc.scalar.copy(window[:], row_arrives_in[i])
-                nc.vector.tensor_tensor(window[:].indirect(offsets[:]), by_cos[:, tokens], by_sin[:, tokens], ADD)
-                nc.sync.dma_start(out_rows[:, i, :], window[:])
+        for u in range(U):
+            for c in range(C):
+                rot = turned.tile([P, B * N], F32, name="rot")
+                nc.tensor.matmul(rot[:], rotate[:].rearrange("k g t e -> k (g t e)"), keys[:, u, c, :], start=True, stop=True)
+                by_cos = products.tile([P, B, N], F32, name="by_cos")
+                by_sin = products.tile([P, B, N], F32, name="by_sin")
+                nc.vector.tensor_tensor(by_cos[:].rearrange("p b j -> p (b j)"), keys[:, u, c, :], cosines[c][:], MULT)
+                nc.vector.tensor_tensor(by_sin[:].rearrange("p b j -> p (b j)"), rot[:], sines[c][:], MULT)
+                for b in range(B):
+                    window = cache.tile([P, S], F32, name="window")
+                    nc.scalar.copy(window[:], arrived[u, c, b])
+                    nc.vector.tensor_tensor(window[:].indirect(offsets[:]), by_cos[:, b, :], by_sin[:, b, :], ADD)
+                    nc.sync.dma_start(out_rows[u, c * B + b], window[:])

@@ -14,6 +14,8 @@ C = 2
 B = 2
 SPAN = 64 // (C * B)
 
+BLOCK = 256
+
 
 def tile_lmattention_kernel(tc, base, k_new, cos_t, sin_t, offs, out):
     nc = tc.nc
@@ -25,25 +27,25 @@ def tile_lmattention_kernel(tc, base, k_new, cos_t, sin_t, offs, out):
         tc.psum_pool(name="spreading", bufs=C) as spreading,
         tc.psum_pool(name="turned", bufs=C) as turned,
     ):
-        factors = held.tile([2 * SPAN, C, B * N], F32, name="factors")
+        factors = held.tile([2 * SPAN, C, B * N], F32, name="factors", align_bytes=BLOCK)
         nc.sync.dma_start(factors[0:SPAN].rearrange("k c f -> k (c f)"), cos_t.rearrange("(k r) j -> k (r j)", r=C * B))
         nc.sync.dma_start(factors[SPAN : 2 * SPAN].rearrange("k c f -> k (c f)"), sin_t.rearrange("(k r) j -> k (r j)", r=C * B))
 
         offsets = held.tile([P, N // 16], U16, name="offsets")
         nc.sync.dma_start(offsets[:], offs)
 
-        keys = held.tile([P, U, C, B * N], F32, name="keys")
+        keys = held.tile([P, U, C, B * N], F32, name="keys", align_bytes=BLOCK)
         nc.sync.dma_start(keys[:].rearrange("p u c f -> p u (c f)"), k_new.rearrange("(u p r) j -> p u (r j)", u=U, r=C * B))
 
         base_rows = base.rearrange("(u p r) s -> u p r s", u=U, r=C * B)
         out_rows = out.rearrange("(u p r) s -> u r p s", u=U, r=C * B)
         arrived = {}
         for c in range(C):
-            pair = held.tile([P, B, S], F32, name=f"pair_{c}")
+            pair = held.tile([P, B, S], F32, name=f"pair_{c}", align_bytes=BLOCK)
             nc.sync.dma_start(pair[:], base_rows[0, :, c * B : (c + 1) * B, :])
             for b in range(B):
                 arrived[0, c, b] = pair[:, b, :]
-        four = held.tile([P, C, B, S], F32, name="four")
+        four = held.tile([P, C, B, S], F32, name="four", align_bytes=BLOCK)
         nc.sync.dma_start(four[:].rearrange("p c b s -> p (c b) s"), base_rows[1])
         for c in range(C):
             for b in range(B):
@@ -83,7 +85,7 @@ def tile_lmattention_kernel(tc, base, k_new, cos_t, sin_t, offs, out):
                 nc.vector.tensor_tensor(by_cos[:].rearrange("p b j -> p (b j)"), keys[:, u, c, :], cosines[c][:], MULT)
                 nc.vector.tensor_tensor(by_sin[:].rearrange("p b j -> p (b j)"), rot[:], sines[c][:], MULT)
                 for b in range(B):
-                    window = cache.tile([P, S], F32, name="window")
+                    window = cache.tile([P, S], F32, name="window", align_bytes=BLOCK)
                     nc.scalar.copy(window[:], arrived[u, c, b])
                     nc.vector.tensor_tensor(window[:].indirect(offsets[:]), by_cos[:, b, :], by_sin[:, b, :], ADD)
                     nc.sync.dma_start(out_rows[u, c * B + b], window[:])

import concourse.mybir as mybir
from concourse.masks import make_identity

F32 = mybir.dt.float32
U16 = mybir.dt.uint16
MULT = mybir.AluOpType.mult
ADD = mybir.AluOpType.add

P = 128
S = 1024
N = 128
U = 2
C = 2
B = 2
SPAN = 64 // (C * B)

BLOCK = 256


def tile_lmattention_kernel(tc, base, k_new, cos_t, sin_t, offs, out):
    nc = tc.nc

    with (
        tc.tile_pool(name="held", bufs=1) as held,
        tc.tile_pool(name="cache", bufs=U * C * B) as cache,
        tc.tile_pool(name="products", bufs=C) as products,
        tc.psum_pool(name="spreading", bufs=C) as spreading,
        tc.psum_pool(name="turned", bufs=C) as turned,
    ):
        factors = held.tile([2 * SPAN, C, B * N], F32, name="factors", align_bytes=BLOCK)
        nc.sync.dma_start(factors[0:SPAN].rearrange("k c f -> k (c f)"), cos_t.rearrange("(k r) j -> k (r j)", r=C * B))
        nc.sync.dma_start(factors[SPAN : 2 * SPAN].rearrange("k c f -> k (c f)"), sin_t.rearrange("(k r) j -> k (r j)", r=C * B))

        offsets = held.tile([P, N // 16], U16, name="offsets")
        nc.sync.dma_start(offsets[:], offs)

        keys = held.tile([P, U, C, B * N], F32, name="keys", align_bytes=BLOCK)
        nc.sync.dma_start(keys[:].rearrange("p u c f -> p u (c f)"), k_new.rearrange("(u p r) j -> p u (r j)", u=U, r=C * B))

        base_rows = base.rearrange("(u p r) s -> u p r s", u=U, r=C * B)
        out_rows = out.rearrange("(u p r) s -> u r p s", u=U, r=C * B)
        arrived = {}
        for c in range(C):
            pair = held.tile([P, B, S], F32, name=f"pair_{c}", align_bytes=BLOCK)
            nc.sync.dma_start(pair[:], base_rows[0, :, c * B : (c + 1) * B, :])
            for b in range(B):
                arrived[0, c, b] = pair[:, b, :]
        four = held.tile([P, C, B, S], F32, name="four", align_bytes=BLOCK)
        nc.sync.dma_start(four[:].rearrange("p c b s -> p (c b) s"), base_rows[1])
        for c in range(C):
            for b in range(B):
                arrived[1, c, b] = four[:, c, b, :]

        identity = held.tile([P, P], F32, name="identity")
        make_identity(nc, identity[:])

        spread_cos = held.tile([2 * SPAN, P // SPAN, SPAN], F32, name="spread_cos")
        spread_sin = held.tile([2 * SPAN, P // SPAN, SPAN], F32, name="spread_sin")
        repeated = [2 * SPAN, P // SPAN, SPAN]
        nc.vector.tensor_copy(spread_cos[:], identity[0 : 2 * SPAN, 0:SPAN].unsqueeze(1).to_broadcast(repeated))
        nc.vector.tensor_copy(spread_sin[:], identity[0 : 2 * SPAN, SPAN : 2 * SPAN].unsqueeze(1).to_broadcast(repeated))

        rotate = held.tile([P, P // (2 * SPAN), 2, SPAN], F32, name="rotate")
        halves = identity[:].rearrange("k (g t e) -> k g t e", t=2, e=SPAN)
        nc.vector.tensor_scalar_mul(rotate[:, :, 0, :], halves[:, :, 1, :], -1.0)
        nc.vector.tensor_copy(rotate[:, :, 1, :], halves[:, :, 0, :])

        cosines, sines = [], []
        for c in range(C):
            cos_spread = spreading.tile([P, B * N], F32, name="cos_spread")
            sin_spread = spreading.tile([P, B * N], F32, name="sin_spread")
            nc.tensor.matmul(cos_spread[:], spread_cos[:].rearrange("k g e -> k (g e)"), factors[:, c, :], start=True, stop=True)
            nc.tensor.matmul(sin_spread[:], spread_sin[:].rearrange("k g e -> k (g e)"), factors[:, c, :], start=True, stop=True)
            sin_here = products.tile([P, B * N], F32, name="sin_here")
            nc.scalar.copy(sin_here[:], sin_spread[:])
            cosines.append(cos_spread)
            sines.append(sin_here)

        for u in range(U):
            for c in range(C):
                rot = turned.tile([P, B * N], F32, name="rot")
                nc.tensor.matmul(rot[:], rotate[:].rearrange("k g t e -> k (g t e)"), keys[:, u, c, :], start=True, stop=True)
                by_cos = products.tile([P, B, N], F32, name="by_cos")
                by_sin = products.tile([P, B, N], F32, name="by_sin")
                nc.vector.tensor_tensor(by_cos[:].rearrange("p b j -> p (b j)"), keys[:, u, c, :], cosines[c][:], MULT)
                nc.vector.tensor_tensor(by_sin[:].rearrange("p b j -> p (b j)"), rot[:], sines[c][:], MULT)
                for b in range(B):
                    window = cache.tile([P, S], F32, name="window", align_bytes=BLOCK)
                    nc.scalar.copy(window[:], arrived[u, c, b])
                    nc.vector.tensor_tensor(window[:].indirect(offsets[:]), by_cos[:, b, :], by_sin[:, b, :], ADD)
                    nc.sync.dma_start(out_rows[u, c * B + b], window[:])
